import numpy as np
import ml_dtypes


def mxq(x, axis, fmt="e4m3"):
    dtype, down = {"e4m3": (ml_dtypes.float8_e4m3fn, 7), "e5m2": (ml_dtypes.float8_e5m2, 14)}[fmt]
    v = np.moveaxis(np.asarray(x, np.float32).astype(ml_dtypes.bfloat16).astype(np.float64), axis, -1)
    blocks = v.reshape(v.shape[:-1] + (-1, 32))
    amax = np.abs(blocks).max(-1, keepdims=True)
    byte = np.maximum(np.where(amax > 0, np.frexp(amax)[1] - 1 + 127, 0) - down, 1)
    scale = np.exp2(byte - 127.0)
    codes = (blocks / scale).astype(np.float32).astype(dtype).astype(np.float64)
    return np.moveaxis((codes * scale).reshape(v.shape), -1, axis)


WIDE = False


def mx_kscale(k):
    if not WIDE:
        return np.ones(k)
    levels = np.array([10, -10, 5, -5, 0])
    a = np.random.permutation(np.resize(levels, k // 512 * 4)).reshape(k // 512, 4)
    idx = np.arange(k)
    return np.exp2(a[idx // 512, idx % 128 // 32])


BF16 = ml_dtypes.bfloat16


def bf(x):
    return np.asarray(x, np.float32).astype(BF16)


def f64(x):
    return np.asarray(x).astype(np.float64)


E2M1 = np.array([0.0, 0.5, 1.0, 1.5, 2.0, 3.0, 4.0, 6.0, -0.0, -0.5, -1.0, -1.5, -2.0, -3.0, -4.0, -6.0])


def pack_weight(w, fmt):
    k, n = w.shape
    w = f64(bf(w)).reshape(k // 32, 32, n)
    amax = np.abs(w).max(1)
    if fmt == "e4m3":
        byte = np.frexp(amax)[1] - 1 + 127 - 7
    else:
        mant, ex = np.frexp(amax / 6.0)
        byte = np.where(mant > 0.5, ex, ex - 1) + 127
    byte = np.clip(np.where(amax > 0, byte, 1), 1, 254)
    scaled = (w * np.exp2(127.0 - byte)[:, None, :]).reshape(k, n).astype(np.float32)
    by_word = np.ascontiguousarray(scaled.reshape(k // 512, 128, 4, n).transpose(0, 1, 3, 2))
    if fmt == "e4m3":
        words = by_word.astype(ml_dtypes.float8_e4m3fn).view(np.uint8)
    else:
        c = by_word.astype(ml_dtypes.float4_e2m1fn).view(np.uint8) & 0xF
        words = c[..., 0::2] | (c[..., 1::2] << 4)
    return np.ascontiguousarray(words), np.ascontiguousarray(byte.astype(np.uint8).reshape(k // 512, 16, n))


def unpack_weight(words, scales, fmt):
    g, p, n, _ = words.shape
    if fmt == "e4m3":
        vals = np.ascontiguousarray(words).view(ml_dtypes.float8_e4m3fn).astype(np.float64)
    else:
        nib = np.empty((g, p, n, 4), np.uint8)
        nib[..., 0::2] = words & 0xF
        nib[..., 1::2] = words >> 4
        vals = E2M1[nib]
    vals = vals * np.repeat(np.exp2(scales.astype(np.float64) - 127.0), 8, axis=1)[..., None]
    return vals.transpose(0, 1, 3, 2).reshape(g * 512, n)


B, L, F, A = 128, 12, 512, 384
E_0, E_1, E_2, E_3, E_4, E_5, E_6, E_7, E_8, E_9, E_10, E_11 = range(1, L + 1)


def setup_inputs():
    s = mx_kscale(L * F).reshape(L, F)
    thresh = 1.0 / (A * L) ** 0.5
    inp = {"x": bf(np.random.standard_normal((B, L, F)) * s)}
    for i in range(L):
        stack = np.random.uniform(-thresh, thresh, (i + 1, F, A)) / s[: i + 1, :, None]
        words, scales = pack_weight(stack.reshape(-1, A), "e4m3")
        inp[f"W_{i}_words"] = words
        inp[f"W_{i}_scales"] = scales
    return inp


def reference(x, W_0_words, W_0_scales, W_1_words, W_1_scales, W_2_words, W_2_scales, W_3_words, W_3_scales, W_4_words, W_4_scales, W_5_words, W_5_scales, W_6_words, W_6_scales, W_7_words, W_7_scales, W_8_words, W_8_scales, W_9_words, W_9_scales, W_10_words, W_10_scales, W_11_words, W_11_scales):
    Ws = [
        unpack_weight(W_0_words, W_0_scales, "e4m3"),
        unpack_weight(W_1_words, W_1_scales, "e4m3"),
        unpack_weight(W_2_words, W_2_scales, "e4m3"),
        unpack_weight(W_3_words, W_3_scales, "e4m3"),
        unpack_weight(W_4_words, W_4_scales, "e4m3"),
        unpack_weight(W_5_words, W_5_scales, "e4m3"),
        unpack_weight(W_6_words, W_6_scales, "e4m3"),
        unpack_weight(W_7_words, W_7_scales, "e4m3"),
        unpack_weight(W_8_words, W_8_scales, "e4m3"),
        unpack_weight(W_9_words, W_9_scales, "e4m3"),
        unpack_weight(W_10_words, W_10_scales, "e4m3"),
        unpack_weight(W_11_words, W_11_scales, "e4m3"),
    ]
    xq = mxq(f64(x).reshape(B, L * F), 1, "e4m3")
    preds = [
        (xq[:, : (i + 1) * F] @ Ws[i].reshape((i + 1) * F, A))
        for i in range(L)
    ]
    return np.stack(preds, axis=1)

@@ -1,0 +1,126 @@
+from contextlib import ExitStack
+
+import concourse.mybir as mybir
+from concourse.masks import make_identity
+
+F32 = mybir.dt.float32
+BF16 = mybir.dt.bfloat16
+I32 = mybir.dt.int32
+U32 = mybir.dt.uint32
+U8 = mybir.dt.uint8
+FP8X4 = mybir.dt.float8_e4m3fn_x4
+
+P = 128
+LAYERS = 12
+F = 512
+A = 384
+PACK = 4
+HALVES = 2
+SCALE_ROWS = 4
+QUADRANTS = 4
+CHUNK = 4
+PAIR = 2
+N_WIDE = 256
+STORE_LAYERS = 4
+
+FLOPS = 2 * P * A * F * (LAYERS * (LAYERS + 1) // 2)
+
+
+def plane_place(i):
+    c = i // QUADRANTS
+    return SCALE_ROWS * (i % QUADRANTS), 2 * c * (c + 1) * A
+
+
+def tile_decoder_pa_e_kernel(tc, x, *weights_and_out):
+    nc = tc.nc
+    words_in = weights_and_out[0 : 2 * LAYERS : 2]
+    scales_in = weights_and_out[1 : 2 * LAYERS : 2]
+    out = weights_and_out[2 * LAYERS]
+    order = list(reversed(range(LAYERS)))
+
+    with ExitStack() as stack:
+        keep = stack.enter_context(tc.tile_pool(name="keep", bufs=1))
+        psum_t = stack.enter_context(tc.psum_pool(name="psum_t", bufs=3))
+        psum_acc = stack.enter_context(tc.psum_pool(name="psum_acc", bufs=4))
+
+        plane_columns = plane_place(LAYERS)[1]
+        planes = keep.tile([P, plane_columns], U8, align_bytes=64)
+        nc.vector.memset(planes[:].bitcast(I32), 0)
+        ident = keep.tile([P, P], F32)
+        make_identity(nc, ident[:])
+
+        x_sb = keep.tile([P, LAYERS, F], BF16)
+        for l0 in range(0, LAYERS, CHUNK):
+            nc.sync.dma_start(out=x_sb[:, l0 : l0 + CHUNK, :], in_=x[:, l0 : l0 + CHUNK, :])
+        w_words = {}
+        for i in order:
+            w_words[i] = keep.tile([P, i + 1, A], U32, name="w_words_%d" % i, align_bytes=64)
+            nc.sync.dma_start(
+                out=w_words[i][:].bitcast(I32),
+                in_=words_in[i].rearrange("g p n t -> p g (n t)").bitcast(I32),
+            )
+        for i in order:
+            k, col = plane_place(i)
+            rows = scales_in[i].bitcast(F32).rearrange("g (q r) n -> r q g n", r=SCALE_ROWS)
+            for r in range(SCALE_ROWS):
+                nc.gpsimd.dma_start(
+                    out=planes[k + r : P : P // QUADRANTS, col : col + (i + 1) * A]
+                    .bitcast(F32)
+                    .rearrange("q (g n) -> q g n", g=i + 1),
+                    in_=rows[r],
+                )
+
+        x_pairs = x_sb[:].rearrange("b l f -> b (l f)").bitcast(F32)
+        pairs_per_layer = F // 2
+        grouped = keep.tile([P, LAYERS, P, PACK], BF16, align_bytes=64)
+        grouped_pairs = (
+            grouped[:]
+            .rearrange("p l b t -> p (l b t)")
+            .bitcast(F32)
+            .rearrange("p (l b u) -> p l b u", l=LAYERS, u=HALVES)
+        )
+        x_codes = keep.tile([P, LAYERS, P], U32, align_bytes=64)
+        x_scales = keep.tile([P, LAYERS, P], U8, align_bytes=64)
+        for l0 in range(0, LAYERS, CHUNK):
+            for l1 in range(l0, l0 + CHUNK, PAIR):
+                xt = psum_t.tile([P, PAIR, HALVES, P], F32)
+                for j in range(PAIR):
+                    first = (l1 + j) * pairs_per_layer
+                    for u in range(HALVES):
+                        nc.tensor.transpose(
+                            xt[:, j, u, :],
+                            x_pairs[:, first + u : first + pairs_per_layer : HALVES],
+                            ident[:],
+                        )
+                copy_out = nc.vector.tensor_copy if (l1 // PAIR) % 2 == 0 else nc.scalar.copy
+                copy_out(
+                    out=grouped_pairs[:, l1 : l1 + PAIR, :, :],
+                    in_=xt[:].rearrange("p j u b -> p j b u"),
+                )
+            nc.vector.quantize_mx(
+                out=x_codes[:, l0 : l0 + CHUNK, :].rearrange("p l b -> p (l b)").bitcast(FP8X4),
+                scales=x_scales[:, l0 : l0 + CHUNK, :].rearrange("p l b -> p (l b)"),
+                in_=grouped[:, l0 : l0 + CHUNK, :, :].rearrange("p l b t -> p (l b t)"),
+            )
+
+        out_sb = keep.tile([P, LAYERS, A], F32)
+        for i in order:
+            k, col = plane_place(i)
+            acc = psum_acc.tile([P, A], F32)
+            for n0, n1 in ((0, N_WIDE), (N_WIDE, A)):
+                for l in range(i + 1):
+                    nc.tensor.matmul_mx(
+                        out=acc[:, n0:n1],
+                        lhsT=x_codes[:, l, :].bitcast(FP8X4),
+                        lhsT_scale=x_scales[:, l, :],
+                        rhs=w_words[i][:, l, n0:n1].bitcast(FP8X4),
+                        rhs_scale=planes[k:P, col + l * A + n0 : col + l * A + n1],
+                        start=(l == 0),
+                        stop=(l == i),
+                    )
+            nc.scalar.copy(out=out_sb[:, i, :], in_=acc[:])
+
+        for i0 in reversed(range(0, LAYERS, STORE_LAYERS)):
+            nc.sync.dma_start(
+                out=out[:, i0 : i0 + STORE_LAYERS, :], in_=out_sb[:, i0 : i0 + STORE_LAYERS, :]
+            )

@@ -26,9 +26,8 @@ STORE_LAYERS = 4
 FLOPS = 2 * P * A * F * (LAYERS * (LAYERS + 1) // 2)
 
 
-def plane_place(i):
-    c = i // QUADRANTS
-    return SCALE_ROWS * (i % QUADRANTS), 2 * c * (c + 1) * A
+def plane_start(i):
+    return SCALE_ROWS * (i % QUADRANTS)
 
 
 def tile_decoder_pa_e_kernel(tc, x, *weights_and_out):
@@ -43,9 +42,6 @@ def tile_decoder_pa_e_kernel(tc, x, *weights_and_out):
         psum_t = stack.enter_context(tc.psum_pool(name="psum_t", bufs=3))
         psum_acc = stack.enter_context(tc.psum_pool(name="psum_acc", bufs=4))
 
-        plane_columns = plane_place(LAYERS)[1]
-        planes = keep.tile([P, plane_columns], U8, align_bytes=64)
-        nc.vector.memset(planes[:].bitcast(I32), 0)
         ident = keep.tile([P, P], F32)
         make_identity(nc, ident[:])
 
@@ -59,15 +55,15 @@ def tile_decoder_pa_e_kernel(tc, x, *weights_and_out):
                 out=w_words[i][:].bitcast(I32),
                 in_=words_in[i].rearrange("g p n t -> p g (n t)").bitcast(I32),
             )
+        w_planes = {}
         for i in order:
-            k, col = plane_place(i)
+            k = plane_start(i)
+            w_planes[i] = keep.tile([P, i + 1, A], U8, name="w_planes_%d" % i, align_bytes=64)
+            nc.vector.memset(w_planes[i][:].rearrange("p g n -> p (g n)").bitcast(I32), 0)
             rows = scales_in[i].bitcast(F32).rearrange("g (q r) n -> r q g n", r=SCALE_ROWS)
             for r in range(SCALE_ROWS):
                 nc.gpsimd.dma_start(
-                    out=planes[k + r : P : P // QUADRANTS, col : col + (i + 1) * A]
-                    .bitcast(F32)
-                    .rearrange("q (g n) -> q g n", g=i + 1),
-                    in_=rows[r],
+                    out=w_planes[i][k + r : P : P // QUADRANTS, :, :].bitcast(F32), in_=rows[r]
                 )
 
         x_pairs = x_sb[:].rearrange("b l f -> b (l f)").bitcast(F32)
@@ -105,7 +101,7 @@ def tile_decoder_pa_e_kernel(tc, x, *weights_and_out):
 
         out_sb = keep.tile([P, LAYERS, A], F32)
         for i in order:
-            k, col = plane_place(i)
+            k = plane_start(i)
             acc = psum_acc.tile([P, A], F32)
             for n0, n1 in ((0, N_WIDE), (N_WIDE, A)):
                 for l in range(i + 1):
@@ -114,7 +110,7 @@ def tile_decoder_pa_e_kernel(tc, x, *weights_and_out):
                         lhsT=x_codes[:, l, :].bitcast(FP8X4),
                         lhsT_scale=x_scales[:, l, :],
                         rhs=w_words[i][:, l, n0:n1].bitcast(FP8X4),
-                        rhs_scale=planes[k:P, col + l * A + n0 : col + l * A + n1],
+                        rhs_scale=w_planes[i][k:P, l, n0:n1],
                         start=(l == 0),
                         stop=(l == i),
                     )

@@ -22,12 +22,19 @@ CHUNK = 4
 PAIR = 2
 N_WIDE = 256
 STORE_LAYERS = 4
+RIDERS = 4
 
 FLOPS = 2 * P * A * F * (LAYERS * (LAYERS + 1) // 2)
 
 
 def plane_start(i):
     return SCALE_ROWS * (i % QUADRANTS)
+
+
+def load_scale_rows(queue, view, planes, scales, k):
+    rows = scales.bitcast(view).rearrange("g (q r) n -> r q g n", r=SCALE_ROWS)
+    for r in range(SCALE_ROWS):
+        queue.dma_start(out=planes[k + r : P : P // QUADRANTS, :, :].bitcast(view), in_=rows[r])
 
 
 def tile_decoder_pa_e_kernel(tc, x, *weights_and_out):
@@ -44,6 +51,10 @@ def tile_decoder_pa_e_kernel(tc, x, *weights_and_out):
 
         ident = keep.tile([P, P], F32)
         make_identity(nc, ident[:])
+        w_planes = {}
+        for i in order:
+            w_planes[i] = keep.tile([P, i + 1, A], U8, name="w_planes_%d" % i, align_bytes=64)
+            nc.vector.memset(w_planes[i][:].rearrange("p g n -> p (g n)").bitcast(I32), 0)
 
         x_sb = keep.tile([P, LAYERS, F], BF16)
         for l0 in range(0, LAYERS, CHUNK):
@@ -55,16 +66,11 @@ def tile_decoder_pa_e_kernel(tc, x, *weights_and_out):
                 out=w_words[i][:].bitcast(I32),
                 in_=words_in[i].rearrange("g p n t -> p g (n t)").bitcast(I32),
             )
-        w_planes = {}
-        for i in order:
-            k = plane_start(i)
-            w_planes[i] = keep.tile([P, i + 1, A], U8, name="w_planes_%d" % i, align_bytes=64)
-            nc.vector.memset(w_planes[i][:].rearrange("p g n -> p (g n)").bitcast(I32), 0)
-            rows = scales_in[i].bitcast(F32).rearrange("g (q r) n -> r q g n", r=SCALE_ROWS)
-            for r in range(SCALE_ROWS):
-                nc.gpsimd.dma_start(
-                    out=w_planes[i][k + r : P : P // QUADRANTS, :, :].bitcast(F32), in_=rows[r]
-                )
+            rider = i - (LAYERS - RIDERS)
+            if rider >= 0:
+                load_scale_rows(nc.sync, I32, w_planes[rider], scales_in[rider], plane_start(rider))
+        for i in order[: LAYERS - RIDERS]:
+            load_scale_rows(nc.gpsimd, F32, w_planes[i], scales_in[i], plane_start(i))
 
         x_pairs = x_sb[:].rearrange("b l f -> b (l f)").bitcast(F32)
         pairs_per_layer = F // 2

@@ -122,7 +122,9 @@ def tile_decoder_pa_e_kernel(tc, x, *weights_and_out):
                     )
             nc.scalar.copy(out=out_sb[:, i, :], in_=acc[:])
 
-        for i0 in reversed(range(0, LAYERS, STORE_LAYERS)):
+        for i0 in reversed(range(STORE_LAYERS, LAYERS, STORE_LAYERS)):
             nc.sync.dma_start(
                 out=out[:, i0 : i0 + STORE_LAYERS, :], in_=out_sb[:, i0 : i0 + STORE_LAYERS, :]
             )
+        for i in reversed(range(STORE_LAYERS)):
+            nc.sync.dma_start(out=out[:, i, :], in_=out_sb[:, i, :])

@@ -23,6 +23,7 @@ PAIR = 2
 N_WIDE = 256
 STORE_LAYERS = 4
 RIDERS = 4
+WORDS_DMA = 4
 
 FLOPS = 2 * P * A * F * (LAYERS * (LAYERS + 1) // 2)
 
@@ -31,10 +32,9 @@ def plane_start(i):
     return SCALE_ROWS * (i % QUADRANTS)
 
 
-def load_scale_rows(queue, view, planes, scales, k):
+def load_scale_row(queue, view, planes, scales, k, r):
     rows = scales.bitcast(view).rearrange("g (q r) n -> r q g n", r=SCALE_ROWS)
-    for r in range(SCALE_ROWS):
-        queue.dma_start(out=planes[k + r : P : P // QUADRANTS, :, :].bitcast(view), in_=rows[r])
+    queue.dma_start(out=planes[k + r : P : P // QUADRANTS, :, :].bitcast(view), in_=rows[r])
 
 
 def tile_decoder_pa_e_kernel(tc, x, *weights_and_out):
@@ -52,25 +52,34 @@ def tile_decoder_pa_e_kernel(tc, x, *weights_and_out):
         ident = keep.tile([P, P], F32)
         make_identity(nc, ident[:])
         w_planes = {}
-        for i in order:
+        for i in range(LAYERS):
             w_planes[i] = keep.tile([P, i + 1, A], U8, name="w_planes_%d" % i, align_bytes=64)
             nc.vector.memset(w_planes[i][:].rearrange("p g n -> p (g n)").bitcast(I32), 0)
 
         x_sb = keep.tile([P, LAYERS, F], BF16)
         for l0 in range(0, LAYERS, CHUNK):
             nc.sync.dma_start(out=x_sb[:, l0 : l0 + CHUNK, :], in_=x[:, l0 : l0 + CHUNK, :])
+        riders = [(i, r) for i in range(RIDERS) for r in range(SCALE_ROWS)]
         w_words = {}
+        pieces = []
         for i in order:
             w_words[i] = keep.tile([P, i + 1, A], U32, name="w_words_%d" % i, align_bytes=64)
-            nc.sync.dma_start(
-                out=w_words[i][:].bitcast(I32),
-                in_=words_in[i].rearrange("g p n t -> p g (n t)").bitcast(I32),
+            pieces.extend(
+                [(i, g0, min(g0 + WORDS_DMA, i + 1)) for g0 in range(0, i + 1, WORDS_DMA)]
             )
-            rider = i - (LAYERS - RIDERS)
-            if rider >= 0:
-                load_scale_rows(nc.sync, I32, w_planes[rider], scales_in[rider], plane_start(rider))
+        for n, (i, g0, g1) in enumerate(pieces):
+            nc.sync.dma_start(
+                out=w_words[i][:, g0:g1, :].bitcast(I32),
+                in_=words_in[i][g0:g1].rearrange("g p n t -> p g (n t)").bitcast(I32),
+            )
+            if n < len(riders):
+                small, r = riders[n]
+                load_scale_row(
+                    nc.sync, I32, w_planes[small], scales_in[small], plane_start(small), r
+                )
         for i in order[: LAYERS - RIDERS]:
-            load_scale_rows(nc.gpsimd, F32, w_planes[i], scales_in[i], plane_start(i))
+            for r in range(SCALE_ROWS):
+                load_scale_row(nc.gpsimd, F32, w_planes[i], scales_in[i], plane_start(i), r)
 
         x_pairs = x_sb[:].rearrange("b l f -> b (l f)").bitcast(F32)
         pairs_per_layer = F // 2
@@ -122,9 +131,7 @@ def tile_decoder_pa_e_kernel(tc, x, *weights_and_out):
                     )
             nc.scalar.copy(out=out_sb[:, i, :], in_=acc[:])
 
-        for i0 in reversed(range(STORE_LAYERS, LAYERS, STORE_LAYERS)):
+        for i0 in reversed(range(0, LAYERS, STORE_LAYERS)):
             nc.sync.dma_start(
                 out=out[:, i0 : i0 + STORE_LAYERS, :], in_=out_sb[:, i0 : i0 + STORE_LAYERS, :]
             )
-        for i in reversed(range(STORE_LAYERS)):
-            nc.sync.dma_start(out=out[:, i, :], in_=out_sb[:, i, :])

@@ -23,6 +23,7 @@ PAIR = 2
 N_WIDE = 256
 STORE_LAYERS = 4
 RIDERS = 4
+DMA_ALIGN = 256
 WORDS_DMA = 4
 
 FLOPS = 2 * P * A * F * (LAYERS * (LAYERS + 1) // 2)
@@ -49,21 +50,25 @@ def tile_decoder_pa_e_kernel(tc, x, *weights_and_out):
         psum_t = stack.enter_context(tc.psum_pool(name="psum_t", bufs=3))
         psum_acc = stack.enter_context(tc.psum_pool(name="psum_acc", bufs=4))
 
-        ident = keep.tile([P, P], F32)
+        ident = keep.tile([P, P], F32, align_bytes=DMA_ALIGN)
         make_identity(nc, ident[:])
         w_planes = {}
         for i in range(LAYERS):
-            w_planes[i] = keep.tile([P, i + 1, A], U8, name="w_planes_%d" % i, align_bytes=64)
+            w_planes[i] = keep.tile(
+                [P, i + 1, A], U8, name="w_planes_%d" % i, align_bytes=DMA_ALIGN
+            )
             nc.vector.memset(w_planes[i][:].rearrange("p g n -> p (g n)").bitcast(I32), 0)
 
-        x_sb = keep.tile([P, LAYERS, F], BF16)
+        x_sb = keep.tile([P, LAYERS, F], BF16, align_bytes=DMA_ALIGN)
         for l0 in range(0, LAYERS, CHUNK):
             nc.sync.dma_start(out=x_sb[:, l0 : l0 + CHUNK, :], in_=x[:, l0 : l0 + CHUNK, :])
         riders = [(i, r) for i in range(RIDERS) for r in range(SCALE_ROWS)]
         w_words = {}
         pieces = []
         for i in order:
-            w_words[i] = keep.tile([P, i + 1, A], U32, name="w_words_%d" % i, align_bytes=64)
+            w_words[i] = keep.tile(
+                [P, i + 1, A], U32, name="w_words_%d" % i, align_bytes=DMA_ALIGN
+            )
             pieces.extend(
                 [(i, g0, min(g0 + WORDS_DMA, i + 1)) for g0 in range(0, i + 1, WORDS_DMA)]
             )
@@ -114,7 +119,7 @@ def tile_decoder_pa_e_kernel(tc, x, *weights_and_out):
                 in_=grouped[:, l0 : l0 + CHUNK, :, :].rearrange("p l b t -> p (l b t)"),
             )
 
-        out_sb = keep.tile([P, LAYERS, A], F32)
+        out_sb = keep.tile([P, LAYERS, A], F32, align_bytes=DMA_ALIGN)
         for i in order:
             k = plane_start(i)
             acc = psum_acc.tile([P, A], F32)

@@ -53,7 +53,7 @@ def tile_decoder_pa_e_kernel(tc, x, *weights_and_out):
         ident = keep.tile([P, P], F32, align_bytes=DMA_ALIGN)
         make_identity(nc, ident[:])
         w_planes = {}
-        for i in range(LAYERS):
+        for i in list(range(RIDERS)) + order[: LAYERS - RIDERS]:
             w_planes[i] = keep.tile(
                 [P, i + 1, A], U8, name="w_planes_%d" % i, align_bytes=DMA_ALIGN
             )

@@ -24,7 +24,7 @@ N_WIDE = 256
 STORE_LAYERS = 4
 RIDERS = 4
 DMA_ALIGN = 256
-WORDS_DMA = 4
+RIDERS_BEHIND = 2
 
 FLOPS = 2 * P * A * F * (LAYERS * (LAYERS + 1) // 2)
 
@@ -64,21 +64,16 @@ def tile_decoder_pa_e_kernel(tc, x, *weights_and_out):
             nc.sync.dma_start(out=x_sb[:, l0 : l0 + CHUNK, :], in_=x[:, l0 : l0 + CHUNK, :])
         riders = [(i, r) for i in range(RIDERS) for r in range(SCALE_ROWS)]
         w_words = {}
-        pieces = []
         for i in order:
             w_words[i] = keep.tile(
                 [P, i + 1, A], U32, name="w_words_%d" % i, align_bytes=DMA_ALIGN
             )
-            pieces.extend(
-                [(i, g0, min(g0 + WORDS_DMA, i + 1)) for g0 in range(0, i + 1, WORDS_DMA)]
-            )
-        for n, (i, g0, g1) in enumerate(pieces):
+        for n, i in enumerate(order):
             nc.sync.dma_start(
-                out=w_words[i][:, g0:g1, :].bitcast(I32),
-                in_=words_in[i][g0:g1].rearrange("g p n t -> p g (n t)").bitcast(I32),
+                out=w_words[i][:].bitcast(I32),
+                in_=words_in[i].rearrange("g p n t -> p g (n t)").bitcast(I32),
             )
-            if n < len(riders):
-                small, r = riders[n]
+            for small, r in riders[n * RIDERS_BEHIND : (n + 1) * RIDERS_BEHIND]:
                 load_scale_row(
                     nc.sync, I32, w_planes[small], scales_in[small], plane_start(small), r
                 )

@@ -22,9 +22,8 @@ CHUNK = 4
 PAIR = 2
 N_WIDE = 256
 STORE_LAYERS = 4
-RIDERS = 4
+RIDERS = 2
 DMA_ALIGN = 256
-RIDERS_BEHIND = 2
 
 FLOPS = 2 * P * A * F * (LAYERS * (LAYERS + 1) // 2)
 
@@ -73,7 +72,8 @@ def tile_decoder_pa_e_kernel(tc, x, *weights_and_out):
                 out=w_words[i][:].bitcast(I32),
                 in_=words_in[i].rearrange("g p n t -> p g (n t)").bitcast(I32),
             )
-            for small, r in riders[n * RIDERS_BEHIND : (n + 1) * RIDERS_BEHIND]:
+            if n < len(riders):
+                small, r = riders[n]
                 load_scale_row(
                     nc.sync, I32, w_planes[small], scales_in[small], plane_start(small), r
                 )

from contextlib import ExitStack

import concourse.mybir as mybir
from concourse.masks import make_identity

F32 = mybir.dt.float32
BF16 = mybir.dt.bfloat16
I32 = mybir.dt.int32
U32 = mybir.dt.uint32
U8 = mybir.dt.uint8
FP8X4 = mybir.dt.float8_e4m3fn_x4

P = 128
LAYERS = 12
F = 512
A = 384
PACK = 4
HALVES = 2
SCALE_ROWS = 4
QUADRANTS = 4
CHUNK = 4
PAIR = 2
N_WIDE = 256
STORE_LAYERS = 4
RIDERS = 2
DMA_ALIGN = 256

FLOPS = 2 * P * A * F * (LAYERS * (LAYERS + 1) // 2)


def plane_start(i):
    return SCALE_ROWS * (i % QUADRANTS)


def load_scale_row(queue, view, planes, scales, k, r):
    rows = scales.bitcast(view).rearrange("g (q r) n -> r q g n", r=SCALE_ROWS)
    queue.dma_start(out=planes[k + r : P : P // QUADRANTS, :, :].bitcast(view), in_=rows[r])


def tile_decoder_pa_e_kernel(tc, x, *weights_and_out):
    nc = tc.nc
    words_in = weights_and_out[0 : 2 * LAYERS : 2]
    scales_in = weights_and_out[1 : 2 * LAYERS : 2]
    out = weights_and_out[2 * LAYERS]
    order = list(reversed(range(LAYERS)))

    with ExitStack() as stack:
        keep = stack.enter_context(tc.tile_pool(name="keep", bufs=1))
        psum_t = stack.enter_context(tc.psum_pool(name="psum_t", bufs=3))
        psum_acc = stack.enter_context(tc.psum_pool(name="psum_acc", bufs=4))

        ident = keep.tile([P, P], F32, align_bytes=DMA_ALIGN)
        make_identity(nc, ident[:])
        w_planes = {}
        for i in list(range(RIDERS)) + order[: LAYERS - RIDERS]:
            w_planes[i] = keep.tile(
                [P, i + 1, A], U8, name="w_planes_%d" % i, align_bytes=DMA_ALIGN
            )
            nc.vector.memset(w_planes[i][:].rearrange("p g n -> p (g n)").bitcast(I32), 0)

        x_sb = keep.tile([P, LAYERS, F], BF16, align_bytes=DMA_ALIGN)
        for l0 in range(0, LAYERS, CHUNK):
            nc.sync.dma_start(out=x_sb[:, l0 : l0 + CHUNK, :], in_=x[:, l0 : l0 + CHUNK, :])
        riders = [(i, r) for i in range(RIDERS) for r in range(SCALE_ROWS)]
        w_words = {}
        for i in order:
            w_words[i] = keep.tile(
                [P, i + 1, A], U32, name="w_words_%d" % i, align_bytes=DMA_ALIGN
            )
        for n, i in enumerate(order):
            nc.sync.dma_start(
                out=w_words[i][:].bitcast(I32),
                in_=words_in[i].rearrange("g p n t -> p g (n t)").bitcast(I32),
            )
            if n < len(riders):
                small, r = riders[n]
                load_scale_row(
                    nc.sync, I32, w_planes[small], scales_in[small], plane_start(small), r
                )
        for i in order[: LAYERS - RIDERS]:
            for r in range(SCALE_ROWS):
                load_scale_row(nc.gpsimd, F32, w_planes[i], scales_in[i], plane_start(i), r)

        x_pairs = x_sb[:].rearrange("b l f -> b (l f)").bitcast(F32)
        pairs_per_layer = F // 2
        grouped = keep.tile([P, LAYERS, P, PACK], BF16, align_bytes=64)
        grouped_pairs = (
            grouped[:]
            .rearrange("p l b t -> p (l b t)")
            .bitcast(F32)
            .rearrange("p (l b u) -> p l b u", l=LAYERS, u=HALVES)
        )
        x_codes = keep.tile([P, LAYERS, P], U32, align_bytes=64)
        x_scales = keep.tile([P, LAYERS, P], U8, align_bytes=64)
        for l0 in range(0, LAYERS, CHUNK):
            for l1 in range(l0, l0 + CHUNK, PAIR):
                xt = psum_t.tile([P, PAIR, HALVES, P], F32)
                for j in range(PAIR):
                    first = (l1 + j) * pairs_per_layer
                    for u in range(HALVES):
                        nc.tensor.transpose(
                            xt[:, j, u, :],
                            x_pairs[:, first + u : first + pairs_per_layer : HALVES],
                            ident[:],
                        )
                copy_out = nc.vector.tensor_copy if (l1 // PAIR) % 2 == 0 else nc.scalar.copy
                copy_out(
                    out=grouped_pairs[:, l1 : l1 + PAIR, :, :],
                    in_=xt[:].rearrange("p j u b -> p j b u"),
                )
            nc.vector.quantize_mx(
                out=x_codes[:, l0 : l0 + CHUNK, :].rearrange("p l b -> p (l b)").bitcast(FP8X4),
                scales=x_scales[:, l0 : l0 + CHUNK, :].rearrange("p l b -> p (l b)"),
                in_=grouped[:, l0 : l0 + CHUNK, :, :].rearrange("p l b t -> p (l b t)"),
            )

        out_sb = keep.tile([P, LAYERS, A], F32, align_bytes=DMA_ALIGN)
        for i in order:
            k = plane_start(i)
            acc = psum_acc.tile([P, A], F32)
            for n0, n1 in ((0, N_WIDE), (N_WIDE, A)):
                for l in range(i + 1):
                    nc.tensor.matmul_mx(
                        out=acc[:, n0:n1],
                        lhsT=x_codes[:, l, :].bitcast(FP8X4),
                        lhsT_scale=x_scales[:, l, :],
                        rhs=w_words[i][:, l, n0:n1].bitcast(FP8X4),
                        rhs_scale=w_planes[i][k:P, l, n0:n1],
                        start=(l == 0),
                        stop=(l == i),
                    )
            nc.scalar.copy(out=out_sb[:, i, :], in_=acc[:])

        for i0 in reversed(range(0, LAYERS, STORE_LAYERS)):
            nc.sync.dma_start(
                out=out[:, i0 : i0 + STORE_LAYERS, :], in_=out_sb[:, i0 : i0 + STORE_LAYERS, :]
            )
